import numpy as np
import ml_dtypes


def mxq(x, axis, fmt="e4m3"):
    dtype, down = {"e4m3": (ml_dtypes.float8_e4m3fn, 7), "e5m2": (ml_dtypes.float8_e5m2, 14)}[fmt]
    v = np.moveaxis(np.asarray(x, np.float32).astype(ml_dtypes.bfloat16).astype(np.float64), axis, -1)
    blocks = v.reshape(v.shape[:-1] + (-1, 32))
    amax = np.abs(blocks).max(-1, keepdims=True)
    byte = np.maximum(np.where(amax > 0, np.frexp(amax)[1] - 1 + 127, 0) - down, 1)
    scale = np.exp2(byte - 127.0)
    codes = (blocks / scale).astype(np.float32).astype(dtype).astype(np.float64)
    return np.moveaxis((codes * scale).reshape(v.shape), -1, axis)


WIDE = False


def mx_kscale(k):
    if not WIDE:
        return np.ones(k)
    levels = np.array([10, -10, 5, -5, 0])
    a = np.random.permutation(np.resize(levels, k // 512 * 4)).reshape(k // 512, 4)
    idx = np.arange(k)
    return np.exp2(a[idx // 512, idx % 128 // 32])


BF16 = ml_dtypes.bfloat16


def bf(x):
    return np.asarray(x, np.float32).astype(BF16)


def f64(x):
    return np.asarray(x).astype(np.float64)


B, T, C, F = 4, 512, 512, 2048
M = T


def silu(v):
    return v / (1.0 + np.exp(-v))


def sigmoid(v):
    return 1.0 / (1.0 + np.exp(-v))


def setup_inputs():
    t = mx_kscale(F)
    x = np.random.standard_normal((B, T, C)) + 0.5 * np.random.standard_normal((B, 1, C))
    return {"h": bf(silu(np.random.standard_normal((B, T, F)) * 0.85) * t),
            "x": bf(x),
            "memory": bf(np.random.standard_normal((1, M, C)) * 6.0 / np.sqrt(C)),
            "w2": bf(np.random.standard_normal((F, C)) * 3.0 / np.sqrt(F) / t[:, None]),
            "b2": bf(np.random.standard_normal(C) * 0.5)}


def reference(h, x, memory, w2, b2):
    update_gate = sigmoid((mxq(f64(h), 2, "e4m3") @ mxq(f64(w2), 0, "e4m3")) + f64(b2))
    x_mean = f64(x).mean(axis=1, keepdims=True)
    new_mem = f64(memory) * (1.0 - update_gate) + x_mean * update_gate
    return new_mem.mean(axis=0, keepdims=True)

@@ -1,0 +1,292 @@
+from contextlib import ExitStack
+
+import concourse.bass as bass
+import concourse.mybir as mybir
+import concourse.tile as tile
+from concourse.masks import make_identity
+
+F32 = mybir.dt.float32
+BF16 = mybir.dt.bfloat16
+U32 = mybir.dt.uint32
+U8 = mybir.dt.uint8
+FP8X4 = mybir.dt.float8_e4m3fn_x4
+ALU = mybir.AluOpType
+ACT = mybir.ActivationFunctionType
+
+P = 128
+B = 4
+T = 512
+C = 512
+F = 2048
+FLOPS = 2 * B * T * F * C
+
+W_GROUPS_ON_VECTOR = 84
+
+
+def tile_dynamicmemorybank_pb_kernel(tc, h, x, memory, w2, b2, out):
+    nc = tc.nc
+    with ExitStack() as ctx:
+        const = ctx.enter_context(tc.tile_pool(name="const", bufs=1))
+        keep = ctx.enter_context(tc.tile_pool(name="keep", bufs=1))
+        work = ctx.enter_context(tc.tile_pool(name="work", bufs=2))
+        ps_acc = ctx.enter_context(tc.psum_pool(name="psacc", bufs=4))
+        ps_tp = ctx.enter_context(tc.psum_pool(name="pstp", bufs=4))
+        ctx.enter_context(tc.manual_schedule())
+
+        ident32 = const.tile([P, P], F32, name="ident32")
+        identb = const.tile([P, P], BF16, name="identb")
+        ones = const.tile([P, 32], BF16, name="ones")
+        b2rows = const.tile([P, P], BF16, name="b2rows")
+        b2col = const.tile([P, 4], F32, name="b2col")
+        warm = const.tile([P, 2], F32, name="warm")
+        make_identity(nc, ident32[:])
+        make_identity(nc, identb[:])
+        nc.vector.memset(b2rows[:], 0.0)
+        nc.vector.memset(ones[:], 1.0)
+        nc.vector.memset(warm[:], 0.0)
+        nc.scalar.dma_start(out=b2rows[0:4, :], in_=b2.rearrange("(r c) -> r c", r=4))
+        nc.scalar.activation(out=warm[:, 1:2], in_=warm[:, 0:1], func=ACT.Sigmoid)
+
+        w_raw = [keep.tile([P, 4 * C], BF16, name="w_raw%d" % g) for g in range(4)]
+        pieces = {}
+        x_sb = [keep.tile([P, 4 * C], BF16, name="x_sb%d" % b) for b in range(B)]
+        mem_sb = keep.tile([P, 4 * C], BF16, name="mem_sb")
+
+        def load_w(g):
+            nc.sync.dma_start(
+                out=w_raw[g][:].rearrange("p (u ec) -> p u ec", u=2),
+                in_=w2[512 * g : 512 * (g + 1), :].rearrange("(u p e) c -> p u (e c)", u=2, e=2),
+            )
+
+        def load_h(b, k0, klen):
+            t = keep.tile([P, 4 * klen], BF16, name="h_%d_%d" % (b, k0))
+            nc.sync.dma_start(
+                out=t[:].rearrange("p (t k) -> p t k", t=4),
+                in_=h[b].rearrange("(p t) k -> p t k", t=4)[:, :, k0 : k0 + klen],
+            )
+            for g in range(k0 // 512, (k0 + klen) // 512):
+                pieces[4 * b + g] = (t, klen, k0)
+
+        def load_x(b):
+            nc.sync.dma_start(out=x_sb[b][:], in_=x[b].rearrange("(p j) c -> p (j c)", j=4))
+
+        for g in range(4):
+            load_w(g)
+            load_h(0, 512 * g, 512)
+        load_h(1, 0, 1024)
+        nc.sync.dma_start(out=mem_sb[:], in_=memory[0].rearrange("(p t) c -> p (t c)", t=4))
+        load_x(0)
+        load_h(1, 1024, 1024)
+        load_h(2, 0, 1024)
+        load_h(2, 1024, 1024)
+        load_x(1)
+        load_h(3, 0, 1024)
+        load_h(3, 1024, 1024)
+        load_x(2)
+        load_x(3)
+
+        wq = keep.tile([P, 4 * C], U32, name="wq", align_bytes=64)
+        ws = keep.tile([P, 4 * C], U8, name="ws", align_bytes=64)
+        memq = keep.tile([P, 4 * T], BF16, name="memq")
+        acc_out = [keep.tile([P, T], F32, name="acc_out%d" % ct) for ct in range(4)]
+        xm4 = [keep.tile([P, 4], F32, name="xm4_%d" % b) for b in range(B)]
+
+        state = {}
+
+        def copy_on(eng, out_ap, in_ap):
+            if eng == "V":
+                nc.vector.tensor_copy(out=out_ap, in_=in_ap)
+            else:
+                nc.scalar.copy(out=out_ap, in_=in_ap)
+
+        def regroup_w(g):
+            gw = work.tile([P, 4 * C], BF16, name="gw", tag="gw", bufs=2, align_bytes=64)
+            state[("gw", g)] = gw
+            dst = gw[:].rearrange("p (c i t) -> p c t i", i=4, t=4)
+            src = w_raw[g][:].rearrange("p (t c i) -> p c t i", t=4, i=4)
+            n = W_GROUPS_ON_VECTOR
+            nc.vector.tensor_copy(out=dst[:, 0:n], in_=src[:, 0:n])
+            nc.scalar.copy(out=dst[:, n:128], in_=src[:, n:128])
+
+        def quant_w(g):
+            nc.vector.quantize_mx(
+                out=wq[:, C * g : C * (g + 1)].bitcast(FP8X4),
+                scales=ws[:, C * g : C * (g + 1)],
+                in_=state[("gw", g)][:],
+            )
+
+        def bias_transpose():
+            pb = ps_tp.tile([P, P], BF16, name="pb", tag="tp")
+            nc.tensor.transpose(out=pb[:], in_=b2rows[:], identity=identb[:])
+            nc.scalar.copy(out=b2col[:], in_=pb[:, 0:4])
+
+        def transposes(u):
+            t, klen, k0 = pieces[u]
+            words = t[:].bitcast(F32)
+            w0 = (512 * (u % 4) - k0) // 2
+            for j in range(2):
+                xt = ps_tp.tile([P, 512], F32, name="xt", tag="tp")
+                state[("xt", u, j)] = xt
+                for tl in range(2):
+                    for uu in range(2):
+                        col = (2 * j + tl) * (klen // 2) + w0 + P * uu
+                        nc.tensor.transpose(
+                            out=xt[:, 256 * uu + P * tl : 256 * uu + P * (tl + 1)],
+                            in_=words[:, col : col + P],
+                            identity=ident32[:],
+                        )
+
+        def evac(u, j, eng):
+            if j == 0:
+                state[("gh", u)] = work.tile([P, 4 * T], BF16, name="gh", tag="gh", bufs=4, align_bytes=64)
+            gh = state[("gh", u)]
+            copy_on(
+                eng,
+                gh[:].bitcast(F32)[:, 512 * j : 512 * (j + 1)].rearrange("p (n u) -> p n u", u=2),
+                state[("xt", u, j)][:].rearrange("p (u n) -> p n u", u=2),
+            )
+
+        def quant_h(u):
+            hq = work.tile([P, T], U32, name="hq", tag="hq", bufs=8, align_bytes=64)
+            hs = work.tile([P, T], U8, name="hs", tag="hs", bufs=8, align_bytes=64)
+            state[("hq", u)] = (hq, hs)
+            nc.vector.quantize_mx(out=hq[:].bitcast(FP8X4), scales=hs[:], in_=state[("gh", u)][:])
+
+        def mx_pass(b, ct, g):
+            n = state.get(("n", b, ct), 0)
+            if n == 0:
+                state[("acc", b, ct)] = ps_acc.tile([P, T], F32, name="acc", tag="acc")
+            state[("n", b, ct)] = n + 1
+            hq, hs = state[("hq", 4 * b + g)]
+            cols = slice(C * g + P * ct, C * g + P * (ct + 1))
+            nc.tensor.matmul_mx(
+                out=state[("acc", b, ct)][:],
+                lhsT=wq[:, cols].bitcast(FP8X4),
+                lhsT_scale=ws[:, cols],
+                rhs=hq[:].bitcast(FP8X4),
+                rhs_scale=hs[:],
+                start=(n == 0),
+                stop=(n == 3),
+            )
+
+        def unit_passes(u):
+            for ct in range(4):
+                mx_pass(u // 4, ct, u % 4)
+
+        def sigmoid(b, ct):
+            gt = work.tile([P, T], F32, name="gt", tag="gt", bufs=8)
+            state[("gt", b, ct)] = gt
+            nc.scalar.activation(
+                out=gt[:], in_=state[("acc", b, ct)][:], func=ACT.Sigmoid, bias=b2col[:, ct : ct + 1], scale=1.0
+            )
+
+        def memory_transposes():
+            for j in range(2):
+                pm = ps_tp.tile([P, 1024], BF16, name="pm", tag="tp")
+                for cl in range(2):
+                    for tt in range(4):
+                        nc.tensor.transpose(
+                            out=pm[:, 512 * cl + P * tt : 512 * cl + P * (tt + 1)],
+                            in_=mem_sb[:, C * tt + P * (2 * j + cl) : C * tt + P * (2 * j + cl + 1)],
+                            identity=identb[:],
+                        )
+                nc.scalar.mul(out=memq[:, 1024 * j : 1024 * (j + 1)], in_=pm[:], mul=0.25)
+
+        def x_sums(b):
+            px = ps_tp.tile([P, P], F32, name="px", tag="tp")
+            for ct in range(4):
+                for j in range(4):
+                    nc.tensor.matmul(
+                        out=px[:, 32 * ct : 32 * (ct + 1)],
+                        lhsT=x_sb[b][:, C * j + P * ct : C * j + P * (ct + 1)],
+                        rhs=ones[:],
+                        start=(j == 0),
+                        stop=(j == 3),
+                    )
+            nc.scalar.mul(
+                out=xm4[b][:].rearrange("p (c o) -> p c o", o=1),
+                in_=px[:].rearrange("p (c n) -> p c n", n=32)[:, :, 0:1],
+                mul=1.0 / (4 * T),
+            )
+
+        def blend(b, ct):
+            mq = memq[:, T * ct : T * (ct + 1)]
+            pr = work.tile([P, T], F32, name="pr", tag="pr", bufs=3)
+            nc.vector.scalar_tensor_tensor(
+                out=pr[:], in0=mq, scalar=xm4[b][:, ct : ct + 1], in1=state[("gt", b, ct)][:],
+                op0=ALU.subtract, op1=ALU.mult,
+            )
+            if b == 0:
+                nc.vector.scalar_tensor_tensor(
+                    out=acc_out[ct][:], in0=mq, scalar=4.0, in1=pr[:], op0=ALU.mult, op1=ALU.subtract
+                )
+            else:
+                nc.vector.tensor_tensor(out=acc_out[ct][:], in0=acc_out[ct][:], in1=pr[:], op=ALU.subtract)
+
+        def finish(ct):
+            pf = ps_tp.tile([P, 512], F32, name="pf", tag="tp")
+            for tt in range(4):
+                nc.tensor.transpose(
+                    out=pf[:, P * tt : P * (tt + 1)], in_=acc_out[ct][:, P * tt : P * (tt + 1)], identity=ident32[:]
+                )
+            ot = work.tile([P, 512], F32, name="ot", tag="ot", bufs=4)
+            nc.scalar.copy(out=ot[:], in_=pf[:])
+            nc.sync.dma_start(
+                out=out[0].rearrange("(p t) c -> p t c", t=4)[:, :, P * ct : P * (ct + 1)],
+                in_=ot[:].rearrange("p (t c) -> p t c", t=4),
+            )
+
+        def evacs(u, e0, e1):
+            evac(u, 0, e0)
+            evac(u, 1, e1)
+
+        regroup_w(0); quant_w(0); bias_transpose()
+        transposes(0); evacs(0, "S", "V"); regroup_w(1); quant_h(0); quant_w(1)
+        transposes(1); evacs(1, "S", "V"); unit_passes(0); regroup_w(2); quant_h(1); quant_w(2)
+        transposes(2); evacs(2, "S", "V"); unit_passes(1); regroup_w(3); quant_h(2); quant_w(3)
+        transposes(3); evacs(3, "S", "V"); unit_passes(2); quant_h(3); unit_passes(3)
+        transposes(4); transposes(5)
+        sigmoid(0, 0); sigmoid(0, 1)
+        evacs(4, "V", "V"); evacs(5, "V", "V")
+        sigmoid(0, 2); sigmoid(0, 3)
+        memory_transposes(); x_sums(0)
+        quant_h(4); quant_h(5)
+        transposes(6); transposes(7)
+        blend(0, 0)
+        evacs(6, "S", "S"); blend(0, 1); evacs(7, "S", "S"); quant_h(6); blend(0, 2); quant_h(7); blend(0, 3)
+        for ct in range(4):
+            mx_pass(1, ct, 0); mx_pass(1, ct, 1)
+        transposes(8); transposes(9); evacs(8, "S", "S"); evacs(9, "S", "S")
+        for ct in (0, 1):
+            mx_pass(1, ct, 2); mx_pass(1, ct, 3); sigmoid(1, ct)
+        quant_h(8); quant_h(9)
+        x_sums(1)
+        transposes(10); transposes(11); evacs(10, "S", "S"); evacs(11, "S", "S")
+        blend(1, 0); blend(1, 1)
+        for ct in (2, 3):
+            mx_pass(1, ct, 2); mx_pass(1, ct, 3); sigmoid(1, ct)
+        quant_h(10); quant_h(11)
+        blend(1, 2); blend(1, 3)
+        transposes(12); transposes(13); evacs(12, "S", "S"); evacs(13, "S", "S")
+        for ct in (0, 1):
+            for g in range(4):
+                mx_pass(2, ct, g)
+            sigmoid(2, ct)
+        quant_h(12); quant_h(13)
+        x_sums(2)
+        blend(2, 0); blend(2, 1)
+        transposes(14); transposes(15); evacs(14, "S", "S"); evacs(15, "S", "S")
+        for ct in (2, 3):
+            for g in range(4):
+                mx_pass(2, ct, g)
+            sigmoid(2, ct)
+        quant_h(14); quant_h(15)
+        x_sums(3)
+        blend(2, 2); blend(2, 3)
+        for ct in range(4):
+            for g in range(4):
+                mx_pass(3, ct, g)
+            sigmoid(3, ct)
+            blend(3, ct)
+        for ct in range(4):
+            finish(ct)

@@ -78,11 +78,11 @@ def tile_dynamicmemorybank_pb_kernel(tc, h, x, memory, w2, b2, out):
         load_x(0)
         load_h(1, 1024, 1024)
         load_h(2, 0, 1024)
-        load_h(2, 1024, 1024)
         load_x(1)
+        load_h(2, 1024, 1024)
         load_h(3, 0, 1024)
-        load_h(3, 1024, 1024)
         load_x(2)
+        load_h(3, 1024, 1024)
         load_x(3)
 
         wq = keep.tile([P, 4 * C], U32, name="wq", align_bytes=64)
@@ -118,7 +118,10 @@ def tile_dynamicmemorybank_pb_kernel(tc, h, x, memory, w2, b2, out):
         def bias_transpose():
             pb = ps_tp.tile([P, P], BF16, name="pb", tag="tp")
             nc.tensor.transpose(out=pb[:], in_=b2rows[:], identity=identb[:])
-            nc.scalar.copy(out=b2col[:], in_=pb[:, 0:4])
+            state["pb"] = pb
+
+        def bias_evac():
+            nc.scalar.copy(out=b2col[:], in_=state["pb"][:, 0:4])
 
         def transposes(u):
             t, klen, k0 = pieces[u]
@@ -209,19 +212,29 @@ def tile_dynamicmemorybank_pb_kernel(tc, h, x, memory, w2, b2, out):
                 mul=1.0 / (4 * T),
             )
 
-        def blend(b, ct):
-            mq = memq[:, T * ct : T * (ct + 1)]
-            pr = work.tile([P, T], F32, name="pr", tag="pr", bufs=3)
+        def blend_mul(b, ct):
+            pr = work.tile([P, T], F32, name="pr", tag="pr", bufs=4)
+            state[("pr", b, ct)] = pr
             nc.vector.scalar_tensor_tensor(
-                out=pr[:], in0=mq, scalar=xm4[b][:, ct : ct + 1], in1=state[("gt", b, ct)][:],
-                op0=ALU.subtract, op1=ALU.mult,
+                out=pr[:], in0=memq[:, T * ct : T * (ct + 1)], scalar=xm4[b][:, ct : ct + 1],
+                in1=state[("gt", b, ct)][:], op0=ALU.subtract, op1=ALU.mult,
             )
+
+        def blend_sub(b, ct):
+            pr = state[("pr", b, ct)]
             if b == 0:
                 nc.vector.scalar_tensor_tensor(
-                    out=acc_out[ct][:], in0=mq, scalar=4.0, in1=pr[:], op0=ALU.mult, op1=ALU.subtract
+                    out=acc_out[ct][:], in0=memq[:, T * ct : T * (ct + 1)], scalar=4.0, in1=pr[:],
+                    op0=ALU.mult, op1=ALU.subtract,
                 )
             else:
                 nc.vector.tensor_tensor(out=acc_out[ct][:], in0=acc_out[ct][:], in1=pr[:], op=ALU.subtract)
+
+        def blend_pair(b, c0, c1):
+            blend_mul(b, c0)
+            blend_mul(b, c1)
+            blend_sub(b, c0)
+            blend_sub(b, c1)
 
         def finish(ct):
             pf = ps_tp.tile([P, 512], F32, name="pf", tag="tp")
@@ -240,53 +253,57 @@ def tile_dynamicmemorybank_pb_kernel(tc, h, x, memory, w2, b2, out):
             evac(u, 0, e0)
             evac(u, 1, e1)
 
-        regroup_w(0); quant_w(0); bias_transpose()
+        regroup_w(0); quant_w(0)
         transposes(0); evacs(0, "S", "V"); regroup_w(1); quant_h(0); quant_w(1)
         transposes(1); evacs(1, "S", "V"); unit_passes(0); regroup_w(2); quant_h(1); quant_w(2)
         transposes(2); evacs(2, "S", "V"); unit_passes(1); regroup_w(3); quant_h(2); quant_w(3)
-        transposes(3); evacs(3, "S", "V"); unit_passes(2); quant_h(3); unit_passes(3)
-        transposes(4); transposes(5)
-        sigmoid(0, 0); sigmoid(0, 1)
-        evacs(4, "V", "V"); evacs(5, "V", "V")
-        sigmoid(0, 2); sigmoid(0, 3)
-        memory_transposes(); x_sums(0)
+        transposes(3); bias_transpose(); evacs(3, "S", "V"); bias_evac(); unit_passes(2); quant_h(3)
+        transposes(4); transposes(5); evacs(4, "S", "V"); evacs(5, "S", "V")
+        unit_passes(3)
         quant_h(4); quant_h(5)
+        sigmoid(0, 0); sigmoid(0, 1)
+        x_sums(0); memory_transposes()
+        sigmoid(0, 2); sigmoid(0, 3)
         transposes(6); transposes(7)
-        blend(0, 0)
-        evacs(6, "S", "S"); blend(0, 1); evacs(7, "S", "S"); quant_h(6); blend(0, 2); quant_h(7); blend(0, 3)
+        blend_pair(0, 0, 1)
+        evacs(6, "S", "S"); evacs(7, "S", "S")
         for ct in range(4):
-            mx_pass(1, ct, 0); mx_pass(1, ct, 1)
-        transposes(8); transposes(9); evacs(8, "S", "S"); evacs(9, "S", "S")
+            mx_pass(1, ct, 0)
+        quant_h(6); quant_h(7)
+        transposes(8); transposes(9)
+        blend_pair(0, 2, 3)
+        evacs(8, "S", "S"); evacs(9, "S", "S")
         for ct in (0, 1):
-            mx_pass(1, ct, 2); mx_pass(1, ct, 3); sigmoid(1, ct)
+            mx_pass(1, ct, 1); mx_pass(1, ct, 2); mx_pass(1, ct, 3); sigmoid(1, ct)
         quant_h(8); quant_h(9)
         x_sums(1)
         transposes(10); transposes(11); evacs(10, "S", "S"); evacs(11, "S", "S")
-        blend(1, 0); blend(1, 1)
+        blend_pair(1, 0, 1)
         for ct in (2, 3):
-            mx_pass(1, ct, 2); mx_pass(1, ct, 3); sigmoid(1, ct)
+            mx_pass(1, ct, 1); mx_pass(1, ct, 2); mx_pass(1, ct, 3); sigmoid(1, ct)
         quant_h(10); quant_h(11)
-        blend(1, 2); blend(1, 3)
         transposes(12); transposes(13); evacs(12, "S", "S"); evacs(13, "S", "S")
+        blend_pair(1, 2, 3)
         for ct in (0, 1):
             for g in range(4):
                 mx_pass(2, ct, g)
             sigmoid(2, ct)
         quant_h(12); quant_h(13)
         x_sums(2)
-        blend(2, 0); blend(2, 1)
         transposes(14); transposes(15); evacs(14, "S", "S"); evacs(15, "S", "S")
+        blend_pair(2, 0, 1)
         for ct in (2, 3):
             for g in range(4):
                 mx_pass(2, ct, g)
             sigmoid(2, ct)
         quant_h(14); quant_h(15)
         x_sums(3)
-        blend(2, 2); blend(2, 3)
+        blend_pair(2, 2, 3)
         for ct in range(4):
             for g in range(4):
                 mx_pass(3, ct, g)
             sigmoid(3, ct)
-            blend(3, ct)
-        for ct in range(4):
-            finish(ct)
+        blend_pair(3, 0, 1)
+        finish(0); finish(1)
+        blend_pair(3, 2, 3)
+        finish(2); finish(3)

@@ -193,7 +193,7 @@ def tile_dynamicmemorybank_pb_kernel(tc, h, x, memory, w2, b2, out):
                             in_=mem_sb[:, C * tt + P * (2 * j + cl) : C * tt + P * (2 * j + cl + 1)],
                             identity=identb[:],
                         )
-                nc.scalar.mul(out=memq[:, 1024 * j : 1024 * (j + 1)], in_=pm[:], mul=0.25)
+                nc.scalar.mul(out=memq[:, 1024 * j : 1024 * (j + 1)], in_=pm[:], mul=-0.25)
 
         def x_sums(b):
             px = ps_tp.tile([P, P], F32, name="px", tag="tp")
@@ -212,23 +212,23 @@ def tile_dynamicmemorybank_pb_kernel(tc, h, x, memory, w2, b2, out):
                 mul=1.0 / (4 * T),
             )
 
-        def blend_mul(b, ct):
-            pr = work.tile([P, T], F32, name="pr", tag="pr", bufs=4)
-            state[("pr", b, ct)] = pr
+        def blend_mul(b, ct, lo=0, hi=T):
+            if lo == 0:
+                state[("pr", b, ct)] = work.tile([P, T], F32, name="pr", tag="pr", bufs=4)
             nc.vector.scalar_tensor_tensor(
-                out=pr[:], in0=memq[:, T * ct : T * (ct + 1)], scalar=xm4[b][:, ct : ct + 1],
-                in1=state[("gt", b, ct)][:], op0=ALU.subtract, op1=ALU.mult,
+                out=state[("pr", b, ct)][:, lo:hi], in0=memq[:, T * ct + lo : T * ct + hi],
+                scalar=xm4[b][:, ct : ct + 1], in1=state[("gt", b, ct)][:, lo:hi], op0=ALU.add, op1=ALU.mult,
             )
 
         def blend_sub(b, ct):
             pr = state[("pr", b, ct)]
             if b == 0:
                 nc.vector.scalar_tensor_tensor(
-                    out=acc_out[ct][:], in0=memq[:, T * ct : T * (ct + 1)], scalar=4.0, in1=pr[:],
-                    op0=ALU.mult, op1=ALU.subtract,
+                    out=acc_out[ct][:], in0=memq[:, T * ct : T * (ct + 1)], scalar=-4.0, in1=pr[:],
+                    op0=ALU.mult, op1=ALU.add,
                 )
             else:
-                nc.vector.tensor_tensor(out=acc_out[ct][:], in0=acc_out[ct][:], in1=pr[:], op=ALU.subtract)
+                nc.vector.tensor_tensor(out=acc_out[ct][:], in0=acc_out[ct][:], in1=pr[:], op=ALU.add)
 
         def blend_pair(b, c0, c1):
             blend_mul(b, c0)
@@ -236,17 +236,22 @@ def tile_dynamicmemorybank_pb_kernel(tc, h, x, memory, w2, b2, out):
             blend_sub(b, c0)
             blend_sub(b, c1)
 
-        def finish(ct):
-            pf = ps_tp.tile([P, 512], F32, name="pf", tag="tp")
-            for tt in range(4):
-                nc.tensor.transpose(
-                    out=pf[:, P * tt : P * (tt + 1)], in_=acc_out[ct][:, P * tt : P * (tt + 1)], identity=ident32[:]
+        def finish_transposes(ct, src, first, last, t0=0, t1=4, pool=ps_tp, tag="tp"):
+            if first:
+                state[("pf", ct, t0)] = pool.tile([P, P * (t1 - t0)], F32, name="pf", tag=tag)
+            pf = state[("pf", ct, t0)]
+            for tt in range(t0, t1):
+                nc.tensor.matmul(
+                    out=pf[:, P * (tt - t0) : P * (tt - t0 + 1)], lhsT=src[:, P * tt : P * (tt + 1)], rhs=ident32[:],
+                    is_transpose=True, start=(first and tt == t0), stop=(last and tt == t1 - 1),
                 )
-            ot = work.tile([P, 512], F32, name="ot", tag="ot", bufs=4)
-            nc.scalar.copy(out=ot[:], in_=pf[:])
+
+        def finish_store(ct, t0=0, t1=4):
+            ot = work.tile([P, P * (t1 - t0)], F32, name="ot", tag="ot", bufs=5)
+            nc.scalar.copy(out=ot[:], in_=state[("pf", ct, t0)][:])
             nc.sync.dma_start(
-                out=out[0].rearrange("(p t) c -> p t c", t=4)[:, :, P * ct : P * (ct + 1)],
-                in_=ot[:].rearrange("p (t c) -> p t c", t=4),
+                out=out[0].rearrange("(p t) c -> p t c", t=4)[:, t0:t1, P * ct : P * (ct + 1)],
+                in_=ot[:].rearrange("p (t c) -> p t c", t=t1 - t0),
             )
 
         def evacs(u, e0, e1):
@@ -303,7 +308,15 @@ def tile_dynamicmemorybank_pb_kernel(tc, h, x, memory, w2, b2, out):
             for g in range(4):
                 mx_pass(3, ct, g)
             sigmoid(3, ct)
+        finish_transposes(2, acc_out[2], True, False)
+        finish_transposes(3, acc_out[3], True, False, 0, 2)
+        finish_transposes(3, acc_out[3], True, False, 2, 4, ps_acc, "acc")
         blend_pair(3, 0, 1)
-        finish(0); finish(1)
-        blend_pair(3, 2, 3)
-        finish(2); finish(3)
+        finish_transposes(0, acc_out[0], True, True); finish_store(0)
+        finish_transposes(1, acc_out[1], True, True); finish_store(1)
+        blend_mul(3, 2)
+        finish_transposes(2, state[("pr", 3, 2)], False, True); finish_store(2)
+        blend_mul(3, 3, 0, 256)
+        finish_transposes(3, state[("pr", 3, 3)], False, True, 0, 2); finish_store(3, 0, 2)
+        blend_mul(3, 3, 256, 512)
+        finish_transposes(3, state[("pr", 3, 3)], False, True, 2, 4); finish_store(3, 2, 4)

@@ -155,19 +155,19 @@ def tile_dynamicmemorybank_pb_kernel(tc, h, x, memory, w2, b2, out):
             state[("hq", u)] = (hq, hs)
             nc.vector.quantize_mx(out=hq[:].bitcast(FP8X4), scales=hs[:], in_=state[("gh", u)][:])
 
-        def mx_pass(b, ct, g):
-            n = state.get(("n", b, ct), 0)
+        def mx_pass(b, ct, g, lo=0, hi=T):
+            n = state.get(("n", b, ct, lo), 0)
             if n == 0:
-                state[("acc", b, ct)] = ps_acc.tile([P, T], F32, name="acc", tag="acc")
-            state[("n", b, ct)] = n + 1
+                state[("acc", b, ct, lo)] = ps_acc.tile([P, hi - lo], F32, name="acc", tag="acc")
+            state[("n", b, ct, lo)] = n + 1
             hq, hs = state[("hq", 4 * b + g)]
             cols = slice(C * g + P * ct, C * g + P * (ct + 1))
             nc.tensor.matmul_mx(
-                out=state[("acc", b, ct)][:],
+                out=state[("acc", b, ct, lo)][:],
                 lhsT=wq[:, cols].bitcast(FP8X4),
                 lhsT_scale=ws[:, cols],
-                rhs=hq[:].bitcast(FP8X4),
-                rhs_scale=hs[:],
+                rhs=hq[:, lo:hi].bitcast(FP8X4),
+                rhs_scale=hs[:, lo:hi],
                 start=(n == 0),
                 stop=(n == 3),
             )
@@ -176,12 +176,21 @@ def tile_dynamicmemorybank_pb_kernel(tc, h, x, memory, w2, b2, out):
             for ct in range(4):
                 mx_pass(u // 4, ct, u % 4)
 
-        def sigmoid(b, ct):
-            gt = work.tile([P, T], F32, name="gt", tag="gt", bufs=8)
-            state[("gt", b, ct)] = gt
+        def sigmoid(b, ct, lo=0, hi=T):
+            if lo == 0:
+                state[("gt", b, ct)] = work.tile([P, T], F32, name="gt", tag="gt", bufs=8)
             nc.scalar.activation(
-                out=gt[:], in_=state[("acc", b, ct)][:], func=ACT.Sigmoid, bias=b2col[:, ct : ct + 1], scale=1.0
+                out=state[("gt", b, ct)][:, lo:hi], in_=state[("acc", b, ct, lo)][:], func=ACT.Sigmoid,
+                bias=b2col[:, ct : ct + 1], scale=1.0,
             )
+
+        def pair_passes(b, c0, c1):
+            for c, g in ((c0, 0), (c0, 1), (c1, 0), (c1, 1), (c0, 2), (c0, 3)):
+                mx_pass(b, c, g)
+            sigmoid(b, c0)
+            mx_pass(b, c1, 2)
+            mx_pass(b, c1, 3)
+            sigmoid(b, c1)
 
         def memory_transposes():
             for j in range(2):
@@ -278,8 +287,10 @@ def tile_dynamicmemorybank_pb_kernel(tc, h, x, memory, w2, b2, out):
         transposes(8); transposes(9)
         blend_pair(0, 2, 3)
         evacs(8, "S", "S"); evacs(9, "S", "S")
-        for ct in (0, 1):
-            mx_pass(1, ct, 1); mx_pass(1, ct, 2); mx_pass(1, ct, 3); sigmoid(1, ct)
+        for g in (1, 2):
+            for ct in (0, 1):
+                mx_pass(1, ct, g)
+        mx_pass(1, 0, 3); sigmoid(1, 0); mx_pass(1, 1, 3); sigmoid(1, 1)
         quant_h(8); quant_h(9)
         x_sums(1)
         transposes(10); transposes(11); evacs(10, "S", "S"); evacs(11, "S", "S")
@@ -289,10 +300,7 @@ def tile_dynamicmemorybank_pb_kernel(tc, h, x, memory, w2, b2, out):
         quant_h(10); quant_h(11)
         transposes(12); transposes(13); evacs(12, "S", "S"); evacs(13, "S", "S")
         blend_pair(1, 2, 3)
-        for ct in (0, 1):
-            for g in range(4):
-                mx_pass(2, ct, g)
-            sigmoid(2, ct)
+        pair_passes(2, 0, 1)
         quant_h(12); quant_h(13)
         x_sums(2)
         transposes(14); transposes(15); evacs(14, "S", "S"); evacs(15, "S", "S")
@@ -304,10 +312,14 @@ def tile_dynamicmemorybank_pb_kernel(tc, h, x, memory, w2, b2, out):
         quant_h(14); quant_h(15)
         x_sums(3)
         blend_pair(2, 2, 3)
-        for ct in range(4):
+        pair_passes(3, 0, 1)
+        for g in range(4):
+            mx_pass(3, 2, g)
+        sigmoid(3, 2)
+        for lo in (0, 256):
             for g in range(4):
-                mx_pass(3, ct, g)
-            sigmoid(3, ct)
+                mx_pass(3, 3, g, lo, lo + 256)
+            sigmoid(3, 3, lo, lo + 256)
         finish_transposes(2, acc_out[2], True, False)
         finish_transposes(3, acc_out[3], True, False, 0, 2)
         finish_transposes(3, acc_out[3], True, False, 2, 4, ps_acc, "acc")

@@ -20,6 +20,7 @@ C = 512
 F = 2048
 FLOPS = 2 * B * T * F * C
 
+W_PAD = 48
 W_GROUPS_ON_VECTOR = 84
 
 
@@ -85,8 +86,8 @@ def tile_dynamicmemorybank_pb_kernel(tc, h, x, memory, w2, b2, out):
         load_h(3, 1024, 1024)
         load_x(3)
 
-        wq = keep.tile([P, 4 * C], U32, name="wq", align_bytes=64)
-        ws = keep.tile([P, 4 * C], U8, name="ws", align_bytes=64)
+        wq = keep.tile([P, W_PAD + 4 * C], U32, name="wq", align_bytes=256)
+        ws = keep.tile([P, 16 * 256], U8, name="ws", align_bytes=256)
         memq = keep.tile([P, 4 * T], BF16, name="memq")
         acc_out = [keep.tile([P, T], F32, name="acc_out%d" % ct) for ct in range(4)]
         xm4 = [keep.tile([P, 4], F32, name="xm4_%d" % b) for b in range(B)]
@@ -109,11 +110,12 @@ def tile_dynamicmemorybank_pb_kernel(tc, h, x, memory, w2, b2, out):
             nc.scalar.copy(out=dst[:, n:128], in_=src[:, n:128])
 
         def quant_w(g):
-            nc.vector.quantize_mx(
-                out=wq[:, C * g : C * (g + 1)].bitcast(FP8X4),
-                scales=ws[:, C * g : C * (g + 1)],
-                in_=state[("gw", g)][:],
-            )
+            for ct in range(4):
+                nc.vector.quantize_mx(
+                    out=wq[:, W_PAD + C * g + P * ct : W_PAD + C * g + P * (ct + 1)].bitcast(FP8X4),
+                    scales=ws[:, 256 * (4 * g + ct) : 256 * (4 * g + ct) + P],
+                    in_=state[("gw", g)][:, 4 * P * ct : 4 * P * (ct + 1)],
+                )
 
         def bias_transpose():
             pb = ps_tp.tile([P, P], BF16, name="pb", tag="tp")
@@ -150,24 +152,23 @@ def tile_dynamicmemorybank_pb_kernel(tc, h, x, memory, w2, b2, out):
             )
 
         def quant_h(u):
-            hq = work.tile([P, T], U32, name="hq", tag="hq", bufs=8, align_bytes=64)
-            hs = work.tile([P, T], U8, name="hs", tag="hs", bufs=8, align_bytes=64)
+            hq = work.tile([P, T], U32, name="hq", tag="hq", bufs=8, align_bytes=256)
+            hs = work.tile([P, T], U8, name="hs", tag="hs", bufs=8, align_bytes=256)
             state[("hq", u)] = (hq, hs)
             nc.vector.quantize_mx(out=hq[:].bitcast(FP8X4), scales=hs[:], in_=state[("gh", u)][:])
 
-        def mx_pass(b, ct, g, lo=0, hi=T):
-            n = state.get(("n", b, ct, lo), 0)
+        def mx_pass(b, ct, g):
+            n = state.get(("n", b, ct), 0)
             if n == 0:
-                state[("acc", b, ct, lo)] = ps_acc.tile([P, hi - lo], F32, name="acc", tag="acc")
-            state[("n", b, ct, lo)] = n + 1
+                state[("acc", b, ct)] = ps_acc.tile([P, T], F32, name="acc", tag="acc")
+            state[("n", b, ct)] = n + 1
             hq, hs = state[("hq", 4 * b + g)]
-            cols = slice(C * g + P * ct, C * g + P * (ct + 1))
             nc.tensor.matmul_mx(
-                out=state[("acc", b, ct, lo)][:],
-                lhsT=wq[:, cols].bitcast(FP8X4),
-                lhsT_scale=ws[:, cols],
-                rhs=hq[:, lo:hi].bitcast(FP8X4),
-                rhs_scale=hs[:, lo:hi],
+                out=state[("acc", b, ct)][:],
+                lhsT=wq[:, W_PAD + C * g + P * ct : W_PAD + C * g + P * (ct + 1)].bitcast(FP8X4),
+                lhsT_scale=ws[:, 256 * (4 * g + ct) : 256 * (4 * g + ct) + P],
+                rhs=hq[:].bitcast(FP8X4),
+                rhs_scale=hs[:],
                 start=(n == 0),
                 stop=(n == 3),
             )
@@ -176,21 +177,12 @@ def tile_dynamicmemorybank_pb_kernel(tc, h, x, memory, w2, b2, out):
             for ct in range(4):
                 mx_pass(u // 4, ct, u % 4)
 
-        def sigmoid(b, ct, lo=0, hi=T):
-            if lo == 0:
-                state[("gt", b, ct)] = work.tile([P, T], F32, name="gt", tag="gt", bufs=8)
+        def sigmoid(b, ct):
+            gt = work.tile([P, T], F32, name="gt", tag="gt", bufs=8)
+            state[("gt", b, ct)] = gt
             nc.scalar.activation(
-                out=state[("gt", b, ct)][:, lo:hi], in_=state[("acc", b, ct, lo)][:], func=ACT.Sigmoid,
-                bias=b2col[:, ct : ct + 1], scale=1.0,
+                out=gt[:], in_=state[("acc", b, ct)][:], func=ACT.Sigmoid, bias=b2col[:, ct : ct + 1], scale=1.0
             )
-
-        def pair_passes(b, c0, c1):
-            for c, g in ((c0, 0), (c0, 1), (c1, 0), (c1, 1), (c0, 2), (c0, 3)):
-                mx_pass(b, c, g)
-            sigmoid(b, c0)
-            mx_pass(b, c1, 2)
-            mx_pass(b, c1, 3)
-            sigmoid(b, c1)
 
         def memory_transposes():
             for j in range(2):
@@ -287,10 +279,8 @@ def tile_dynamicmemorybank_pb_kernel(tc, h, x, memory, w2, b2, out):
         transposes(8); transposes(9)
         blend_pair(0, 2, 3)
         evacs(8, "S", "S"); evacs(9, "S", "S")
-        for g in (1, 2):
-            for ct in (0, 1):
-                mx_pass(1, ct, g)
-        mx_pass(1, 0, 3); sigmoid(1, 0); mx_pass(1, 1, 3); sigmoid(1, 1)
+        for ct in (0, 1):
+            mx_pass(1, ct, 1); mx_pass(1, ct, 2); mx_pass(1, ct, 3); sigmoid(1, ct)
         quant_h(8); quant_h(9)
         x_sums(1)
         transposes(10); transposes(11); evacs(10, "S", "S"); evacs(11, "S", "S")
@@ -300,7 +290,10 @@ def tile_dynamicmemorybank_pb_kernel(tc, h, x, memory, w2, b2, out):
         quant_h(10); quant_h(11)
         transposes(12); transposes(13); evacs(12, "S", "S"); evacs(13, "S", "S")
         blend_pair(1, 2, 3)
-        pair_passes(2, 0, 1)
+        for ct in (0, 1):
+            for g in range(4):
+                mx_pass(2, ct, g)
+            sigmoid(2, ct)
         quant_h(12); quant_h(13)
         x_sums(2)
         transposes(14); transposes(15); evacs(14, "S", "S"); evacs(15, "S", "S")
@@ -312,14 +305,10 @@ def tile_dynamicmemorybank_pb_kernel(tc, h, x, memory, w2, b2, out):
         quant_h(14); quant_h(15)
         x_sums(3)
         blend_pair(2, 2, 3)
-        pair_passes(3, 0, 1)
-        for g in range(4):
-            mx_pass(3, 2, g)
-        sigmoid(3, 2)
-        for lo in (0, 256):
+        for ct in range(4):
             for g in range(4):
-                mx_pass(3, 3, g, lo, lo + 256)
-            sigmoid(3, 3, lo, lo + 256)
+                mx_pass(3, ct, g)
+            sigmoid(3, ct)
         finish_transposes(2, acc_out[2], True, False)
         finish_transposes(3, acc_out[3], True, False, 0, 2)
         finish_transposes(3, acc_out[3], True, False, 2, 4, ps_acc, "acc")

from contextlib import ExitStack

import concourse.bass as bass
import concourse.mybir as mybir
import concourse.tile as tile
from concourse.masks import make_identity

F32 = mybir.dt.float32
BF16 = mybir.dt.bfloat16
U32 = mybir.dt.uint32
U8 = mybir.dt.uint8
FP8X4 = mybir.dt.float8_e4m3fn_x4
ALU = mybir.AluOpType
ACT = mybir.ActivationFunctionType

P = 128
B = 4
T = 512
C = 512
F = 2048
FLOPS = 2 * B * T * F * C

W_PAD = 48
W_GROUPS_ON_VECTOR = 84


def tile_dynamicmemorybank_pb_kernel(tc, h, x, memory, w2, b2, out):
    nc = tc.nc
    with ExitStack() as ctx:
        const = ctx.enter_context(tc.tile_pool(name="const", bufs=1))
        keep = ctx.enter_context(tc.tile_pool(name="keep", bufs=1))
        work = ctx.enter_context(tc.tile_pool(name="work", bufs=2))
        ps_acc = ctx.enter_context(tc.psum_pool(name="psacc", bufs=4))
        ps_tp = ctx.enter_context(tc.psum_pool(name="pstp", bufs=4))
        ctx.enter_context(tc.manual_schedule())

        ident32 = const.tile([P, P], F32, name="ident32")
        identb = const.tile([P, P], BF16, name="identb")
        ones = const.tile([P, 32], BF16, name="ones")
        b2rows = const.tile([P, P], BF16, name="b2rows")
        b2col = const.tile([P, 4], F32, name="b2col")
        warm = const.tile([P, 2], F32, name="warm")
        make_identity(nc, ident32[:])
        make_identity(nc, identb[:])
        nc.vector.memset(b2rows[:], 0.0)
        nc.vector.memset(ones[:], 1.0)
        nc.vector.memset(warm[:], 0.0)
        nc.scalar.dma_start(out=b2rows[0:4, :], in_=b2.rearrange("(r c) -> r c", r=4))
        nc.scalar.activation(out=warm[:, 1:2], in_=warm[:, 0:1], func=ACT.Sigmoid)

        w_raw = [keep.tile([P, 4 * C], BF16, name="w_raw%d" % g) for g in range(4)]
        pieces = {}
        x_sb = [keep.tile([P, 4 * C], BF16, name="x_sb%d" % b) for b in range(B)]
        mem_sb = keep.tile([P, 4 * C], BF16, name="mem_sb")

        def load_w(g):
            nc.sync.dma_start(
                out=w_raw[g][:].rearrange("p (u ec) -> p u ec", u=2),
                in_=w2[512 * g : 512 * (g + 1), :].rearrange("(u p e) c -> p u (e c)", u=2, e=2),
            )

        def load_h(b, k0, klen):
            t = keep.tile([P, 4 * klen], BF16, name="h_%d_%d" % (b, k0))
            nc.sync.dma_start(
                out=t[:].rearrange("p (t k) -> p t k", t=4),
                in_=h[b].rearrange("(p t) k -> p t k", t=4)[:, :, k0 : k0 + klen],
            )
            for g in range(k0 // 512, (k0 + klen) // 512):
                pieces[4 * b + g] = (t, klen, k0)

        def load_x(b):
            nc.sync.dma_start(out=x_sb[b][:], in_=x[b].rearrange("(p j) c -> p (j c)", j=4))

        for g in range(4):
            load_w(g)
            load_h(0, 512 * g, 512)
        load_h(1, 0, 1024)
        nc.sync.dma_start(out=mem_sb[:], in_=memory[0].rearrange("(p t) c -> p (t c)", t=4))
        load_x(0)
        load_h(1, 1024, 1024)
        load_h(2, 0, 1024)
        load_x(1)
        load_h(2, 1024, 1024)
        load_h(3, 0, 1024)
        load_x(2)
        load_h(3, 1024, 1024)
        load_x(3)

        wq = keep.tile([P, W_PAD + 4 * C], U32, name="wq", align_bytes=256)
        ws = keep.tile([P, 16 * 256], U8, name="ws", align_bytes=256)
        memq = keep.tile([P, 4 * T], BF16, name="memq")
        acc_out = [keep.tile([P, T], F32, name="acc_out%d" % ct) for ct in range(4)]
        xm4 = [keep.tile([P, 4], F32, name="xm4_%d" % b) for b in range(B)]

        state = {}

        def copy_on(eng, out_ap, in_ap):
            if eng == "V":
                nc.vector.tensor_copy(out=out_ap, in_=in_ap)
            else:
                nc.scalar.copy(out=out_ap, in_=in_ap)

        def regroup_w(g):
            gw = work.tile([P, 4 * C], BF16, name="gw", tag="gw", bufs=2, align_bytes=64)
            state[("gw", g)] = gw
            dst = gw[:].rearrange("p (c i t) -> p c t i", i=4, t=4)
            src = w_raw[g][:].rearrange("p (t c i) -> p c t i", t=4, i=4)
            n = W_GROUPS_ON_VECTOR
            nc.vector.tensor_copy(out=dst[:, 0:n], in_=src[:, 0:n])
            nc.scalar.copy(out=dst[:, n:128], in_=src[:, n:128])

        def quant_w(g):
            for ct in range(4):
                nc.vector.quantize_mx(
                    out=wq[:, W_PAD + C * g + P * ct : W_PAD + C * g + P * (ct + 1)].bitcast(FP8X4),
                    scales=ws[:, 256 * (4 * g + ct) : 256 * (4 * g + ct) + P],
                    in_=state[("gw", g)][:, 4 * P * ct : 4 * P * (ct + 1)],
                )

        def bias_transpose():
            pb = ps_tp.tile([P, P], BF16, name="pb", tag="tp")
            nc.tensor.transpose(out=pb[:], in_=b2rows[:], identity=identb[:])
            state["pb"] = pb

        def bias_evac():
            nc.scalar.copy(out=b2col[:], in_=state["pb"][:, 0:4])

        def transposes(u):
            t, klen, k0 = pieces[u]
            words = t[:].bitcast(F32)
            w0 = (512 * (u % 4) - k0) // 2
            for j in range(2):
                xt = ps_tp.tile([P, 512], F32, name="xt", tag="tp")
                state[("xt", u, j)] = xt
                for tl in range(2):
                    for uu in range(2):
                        col = (2 * j + tl) * (klen // 2) + w0 + P * uu
                        nc.tensor.transpose(
                            out=xt[:, 256 * uu + P * tl : 256 * uu + P * (tl + 1)],
                            in_=words[:, col : col + P],
                            identity=ident32[:],
                        )

        def evac(u, j, eng):
            if j == 0:
                state[("gh", u)] = work.tile([P, 4 * T], BF16, name="gh", tag="gh", bufs=4, align_bytes=64)
            gh = state[("gh", u)]
            copy_on(
                eng,
                gh[:].bitcast(F32)[:, 512 * j : 512 * (j + 1)].rearrange("p (n u) -> p n u", u=2),
                state[("xt", u, j)][:].rearrange("p (u n) -> p n u", u=2),
            )

        def quant_h(u):
            hq = work.tile([P, T], U32, name="hq", tag="hq", bufs=8, align_bytes=256)
            hs = work.tile([P, T], U8, name="hs", tag="hs", bufs=8, align_bytes=256)
            state[("hq", u)] = (hq, hs)
            nc.vector.quantize_mx(out=hq[:].bitcast(FP8X4), scales=hs[:], in_=state[("gh", u)][:])

        def mx_pass(b, ct, g):
            n = state.get(("n", b, ct), 0)
            if n == 0:
                state[("acc", b, ct)] = ps_acc.tile([P, T], F32, name="acc", tag="acc")
            state[("n", b, ct)] = n + 1
            hq, hs = state[("hq", 4 * b + g)]
            nc.tensor.matmul_mx(
                out=state[("acc", b, ct)][:],
                lhsT=wq[:, W_PAD + C * g + P * ct : W_PAD + C * g + P * (ct + 1)].bitcast(FP8X4),
                lhsT_scale=ws[:, 256 * (4 * g + ct) : 256 * (4 * g + ct) + P],
                rhs=hq[:].bitcast(FP8X4),
                rhs_scale=hs[:],
                start=(n == 0),
                stop=(n == 3),
            )

        def unit_passes(u):
            for ct in range(4):
                mx_pass(u // 4, ct, u % 4)

        def sigmoid(b, ct):
            gt = work.tile([P, T], F32, name="gt", tag="gt", bufs=8)
            state[("gt", b, ct)] = gt
            nc.scalar.activation(
                out=gt[:], in_=state[("acc", b, ct)][:], func=ACT.Sigmoid, bias=b2col[:, ct : ct + 1], scale=1.0
            )

        def memory_transposes():
            for j in range(2):
                pm = ps_tp.tile([P, 1024], BF16, name="pm", tag="tp")
                for cl in range(2):
                    for tt in range(4):
                        nc.tensor.transpose(
                            out=pm[:, 512 * cl + P * tt : 512 * cl + P * (tt + 1)],
                            in_=mem_sb[:, C * tt + P * (2 * j + cl) : C * tt + P * (2 * j + cl + 1)],
                            identity=identb[:],
                        )
                nc.scalar.mul(out=memq[:, 1024 * j : 1024 * (j + 1)], in_=pm[:], mul=-0.25)

        def x_sums(b):
            px = ps_tp.tile([P, P], F32, name="px", tag="tp")
            for ct in range(4):
                for j in range(4):
                    nc.tensor.matmul(
                        out=px[:, 32 * ct : 32 * (ct + 1)],
                        lhsT=x_sb[b][:, C * j + P * ct : C * j + P * (ct + 1)],
                        rhs=ones[:],
                        start=(j == 0),
                        stop=(j == 3),
                    )
            nc.scalar.mul(
                out=xm4[b][:].rearrange("p (c o) -> p c o", o=1),
                in_=px[:].rearrange("p (c n) -> p c n", n=32)[:, :, 0:1],
                mul=1.0 / (4 * T),
            )

        def blend_mul(b, ct, lo=0, hi=T):
            if lo == 0:
                state[("pr", b, ct)] = work.tile([P, T], F32, name="pr", tag="pr", bufs=4)
            nc.vector.scalar_tensor_tensor(
                out=state[("pr", b, ct)][:, lo:hi], in0=memq[:, T * ct + lo : T * ct + hi],
                scalar=xm4[b][:, ct : ct + 1], in1=state[("gt", b, ct)][:, lo:hi], op0=ALU.add, op1=ALU.mult,
            )

        def blend_sub(b, ct):
            pr = state[("pr", b, ct)]
            if b == 0:
                nc.vector.scalar_tensor_tensor(
                    out=acc_out[ct][:], in0=memq[:, T * ct : T * (ct + 1)], scalar=-4.0, in1=pr[:],
                    op0=ALU.mult, op1=ALU.add,
                )
            else:
                nc.vector.tensor_tensor(out=acc_out[ct][:], in0=acc_out[ct][:], in1=pr[:], op=ALU.add)

        def blend_pair(b, c0, c1):
            blend_mul(b, c0)
            blend_mul(b, c1)
            blend_sub(b, c0)
            blend_sub(b, c1)

        def finish_transposes(ct, src, first, last, t0=0, t1=4, pool=ps_tp, tag="tp"):
            if first:
                state[("pf", ct, t0)] = pool.tile([P, P * (t1 - t0)], F32, name="pf", tag=tag)
            pf = state[("pf", ct, t0)]
            for tt in range(t0, t1):
                nc.tensor.matmul(
                    out=pf[:, P * (tt - t0) : P * (tt - t0 + 1)], lhsT=src[:, P * tt : P * (tt + 1)], rhs=ident32[:],
                    is_transpose=True, start=(first and tt == t0), stop=(last and tt == t1 - 1),
                )

        def finish_store(ct, t0=0, t1=4):
            ot = work.tile([P, P * (t1 - t0)], F32, name="ot", tag="ot", bufs=5)
            nc.scalar.copy(out=ot[:], in_=state[("pf", ct, t0)][:])
            nc.sync.dma_start(
                out=out[0].rearrange("(p t) c -> p t c", t=4)[:, t0:t1, P * ct : P * (ct + 1)],
                in_=ot[:].rearrange("p (t c) -> p t c", t=t1 - t0),
            )

        def evacs(u, e0, e1):
            evac(u, 0, e0)
            evac(u, 1, e1)

        regroup_w(0); quant_w(0)
        transposes(0); evacs(0, "S", "V"); regroup_w(1); quant_h(0); quant_w(1)
        transposes(1); evacs(1, "S", "V"); unit_passes(0); regroup_w(2); quant_h(1); quant_w(2)
        transposes(2); evacs(2, "S", "V"); unit_passes(1); regroup_w(3); quant_h(2); quant_w(3)
        transposes(3); bias_transpose(); evacs(3, "S", "V"); bias_evac(); unit_passes(2); quant_h(3)
        transposes(4); transposes(5); evacs(4, "S", "V"); evacs(5, "S", "V")
        unit_passes(3)
        quant_h(4); quant_h(5)
        sigmoid(0, 0); sigmoid(0, 1)
        x_sums(0); memory_transposes()
        sigmoid(0, 2); sigmoid(0, 3)
        transposes(6); transposes(7)
        blend_pair(0, 0, 1)
        evacs(6, "S", "S"); evacs(7, "S", "S")
        for ct in range(4):
            mx_pass(1, ct, 0)
        quant_h(6); quant_h(7)
        transposes(8); transposes(9)
        blend_pair(0, 2, 3)
        evacs(8, "S", "S"); evacs(9, "S", "S")
        for ct in (0, 1):
            mx_pass(1, ct, 1); mx_pass(1, ct, 2); mx_pass(1, ct, 3); sigmoid(1, ct)
        quant_h(8); quant_h(9)
        x_sums(1)
        transposes(10); transposes(11); evacs(10, "S", "S"); evacs(11, "S", "S")
        blend_pair(1, 0, 1)
        for ct in (2, 3):
            mx_pass(1, ct, 1); mx_pass(1, ct, 2); mx_pass(1, ct, 3); sigmoid(1, ct)
        quant_h(10); quant_h(11)
        transposes(12); transposes(13); evacs(12, "S", "S"); evacs(13, "S", "S")
        blend_pair(1, 2, 3)
        for ct in (0, 1):
            for g in range(4):
                mx_pass(2, ct, g)
            sigmoid(2, ct)
        quant_h(12); quant_h(13)
        x_sums(2)
        transposes(14); transposes(15); evacs(14, "S", "S"); evacs(15, "S", "S")
        blend_pair(2, 0, 1)
        for ct in (2, 3):
            for g in range(4):
                mx_pass(2, ct, g)
            sigmoid(2, ct)
        quant_h(14); quant_h(15)
        x_sums(3)
        blend_pair(2, 2, 3)
        for ct in range(4):
            for g in range(4):
                mx_pass(3, ct, g)
            sigmoid(3, ct)
        finish_transposes(2, acc_out[2], True, False)
        finish_transposes(3, acc_out[3], True, False, 0, 2)
        finish_transposes(3, acc_out[3], True, False, 2, 4, ps_acc, "acc")
        blend_pair(3, 0, 1)
        finish_transposes(0, acc_out[0], True, True); finish_store(0)
        finish_transposes(1, acc_out[1], True, True); finish_store(1)
        blend_mul(3, 2)
        finish_transposes(2, state[("pr", 3, 2)], False, True); finish_store(2)
        blend_mul(3, 3, 0, 256)
        finish_transposes(3, state[("pr", 3, 3)], False, True, 0, 2); finish_store(3, 0, 2)
        blend_mul(3, 3, 256, 512)
        finish_transposes(3, state[("pr", 3, 3)], False, True, 2, 4); finish_store(3, 2, 4)
